import numpy as np
import ml_dtypes


BF16 = ml_dtypes.bfloat16


def bf(x):
    return np.asarray(x, np.float32).astype(BF16)


def f64(x):
    return np.asarray(x).astype(np.float64)


E2M1 = np.array([0.0, 0.5, 1.0, 1.5, 2.0, 3.0, 4.0, 6.0, -0.0, -0.5, -1.0, -1.5, -2.0, -3.0, -4.0, -6.0])


def pack_weight(w, fmt):
    k, n = w.shape
    w = f64(bf(w)).reshape(k // 32, 32, n)
    amax = np.abs(w).max(1)
    if fmt == "e4m3":
        byte = np.frexp(amax)[1] - 1 + 127 - 7
    else:
        mant, ex = np.frexp(amax / 6.0)
        byte = np.where(mant > 0.5, ex, ex - 1) + 127
    byte = np.clip(np.where(amax > 0, byte, 1), 1, 254)
    scaled = (w * np.exp2(127.0 - byte)[:, None, :]).reshape(k, n).astype(np.float32)
    by_word = np.ascontiguousarray(scaled.reshape(k // 512, 128, 4, n).transpose(0, 1, 3, 2))
    if fmt == "e4m3":
        words = by_word.astype(ml_dtypes.float8_e4m3fn).view(np.uint8)
    else:
        c = by_word.astype(ml_dtypes.float4_e2m1fn).view(np.uint8) & 0xF
        words = c[..., 0::2] | (c[..., 1::2] << 4)
    return np.ascontiguousarray(words), np.ascontiguousarray(byte.astype(np.uint8).reshape(k // 512, 16, n))


def unpack_weight(words, scales, fmt):
    g, p, n, _ = words.shape
    if fmt == "e4m3":
        vals = np.ascontiguousarray(words).view(ml_dtypes.float8_e4m3fn).astype(np.float64)
    else:
        nib = np.empty((g, p, n, 4), np.uint8)
        nib[..., 0::2] = words & 0xF
        nib[..., 1::2] = words >> 4
        vals = E2M1[nib]
    vals = vals * np.repeat(np.exp2(scales.astype(np.float64) - 127.0), 8, axis=1)[..., None]
    return vals.transpose(0, 1, 3, 2).reshape(g * 512, n)

def pack4(w):
    words, scales = pack_weight(w, "e2m1")
    return words.reshape(words.shape[0], 128, -1), scales


def unpack4(words, scales):
    return unpack_weight(words.reshape(words.shape[0], 128, -1, 2), scales, "e2m1")


def kspread(k):
    return np.exp2(np.repeat(np.random.randint(-6, 7, k // 32), 32).astype(np.float64))


B, T, C, HQ, HKV, HD = 4, 512, 4096, 16, 4, 128
EPS = 1e-6


def apply_rope(u, cos, sin):
    c = cos[None, :, None, :]
    s = sin[None, :, None, :]
    u1, u2 = u[..., ::2], u[..., 1::2]
    return np.concatenate([u1 * c - u2 * s, u1 * s + u2 * c], axis=-1)


def rmsnorm(u, w):
    return w * (u / np.sqrt(np.mean(u * u, axis=-1, keepdims=True) + EPS))


def setup_inputs():
    s = kspread(C)
    inv_freq = 1.0 / (10000.0 ** (np.arange(0, HD, 2) / HD))
    freqs = np.arange(T)[:, None] * inv_freq[None, :]
    x = np.random.standard_normal((B, T, C)) * s
    x_words, x_scales = pack4(np.ascontiguousarray(x.reshape(B * T, C).T))
    Wq_words, Wq_scales = pack4(np.ascontiguousarray((np.random.standard_normal((HQ * HD, C)) / np.sqrt(C) / s).T))
    bq = bf(np.random.standard_normal(HQ * HD) * 0.3)
    Wk_words, Wk_scales = pack4(np.ascontiguousarray((np.random.standard_normal((HKV * HD, C)) / np.sqrt(C) / s).T))
    bk = bf(np.random.standard_normal(HKV * HD) * 0.3)
    return {"x_words": x_words,
            "x_scales": x_scales,
            "Wq_words": Wq_words,
            "Wq_scales": Wq_scales,
            "bq": bq,
            "Wk_words": Wk_words,
            "Wk_scales": Wk_scales,
            "bk": bk,
            "qn_w": bf(1.0 + 0.1 * np.random.standard_normal(HD)),
            "kn_w": bf(1.0 + 0.1 * np.random.standard_normal(HD)),
            "cos": bf(np.cos(freqs)),
            "sin": bf(np.sin(freqs))}


def reference(x_words, x_scales, Wq_words, Wq_scales, bq, Wk_words, Wk_scales, bk, qn_w, kn_w, cos, sin):
    xq = unpack4(x_words, x_scales).T.reshape(B * T, C)
    q = ((xq @ unpack4(Wq_words, Wq_scales)) + f64(bq)).reshape(B, T, HQ, HD)
    k = ((xq @ unpack4(Wk_words, Wk_scales)) + f64(bk)).reshape(B, T, HKV, HD)
    q = rmsnorm(apply_rope(q, f64(cos), f64(sin)), f64(qn_w))
    k = rmsnorm(apply_rope(k, f64(cos), f64(sin)), f64(kn_w))
    return q, k

@@ -1,0 +1,307 @@
+from contextlib import ExitStack
+
+import concourse.mybir as mybir
+from concourse.masks import make_identity
+
+FLOPS = 2 * 2048 * 4096 * 2560
+
+F32 = mybir.dt.float32
+BF16 = mybir.dt.bfloat16
+U8 = mybir.dt.uint8
+I32 = mybir.dt.int32
+FP4X4 = mybir.dt.float4_e2m1fn_x4
+ALU = mybir.AluOpType
+ACT = mybir.ActivationFunctionType
+
+P = 128
+PASSES = 8
+BLOCKS = 4
+BANKS = 5
+EPS = 1e-6
+
+
+def tile_gqaselfattention_pa_kernel(
+    tc, x_words, x_scales, Wq_words, Wq_scales, bq, Wk_words, Wk_scales, bk, qn_w, kn_w, cos, sin, out_0, out_1
+):
+    nc = tc.nc
+    q_rows = out_0.rearrange("b t h d -> (b t) (h d)")
+    k_rows = out_1.rearrange("b t h d -> (b t) (h d)")
+
+    with ExitStack() as ctx:
+        keep = ctx.enter_context(tc.tile_pool(name="keep", bufs=1))
+        work = ctx.enter_context(tc.tile_pool(name="work", bufs=2))
+        acc_pool = ctx.enter_context(tc.psum_pool(name="acc", bufs=7))
+        tab_pool = ctx.enter_context(tc.psum_pool(name="tab", bufs=1))
+        ctx.enter_context(tc.manual_schedule())
+
+        def make_run(name, g0, g1):
+            codes = keep.tile([P, g1 - g0, 1024], U8, name=name + "c", tag=name + "c", align_bytes=64)
+            planes = keep.tile([P, g1 - g0, 512], U8, name=name + "s", tag=name + "s", align_bytes=64)
+            nc.vector.memset(planes[:].bitcast(I32), 0)
+            return (g0, g1, codes, planes)
+
+        def load_codes(run, words):
+            g0, g1, codes, planes = run
+            nc.sync.dma_start(
+                out=codes[:].bitcast(I32), in_=words[g0:g1].rearrange("g p n -> p g n").bitcast(I32)
+            )
+
+        def load_scales(run, scales):
+            g0, g1, codes, planes = run
+            for q in range(4):
+                nc.sync.dma_start(
+                    out=planes[32 * q : 32 * q + 4, :, :].bitcast(I32),
+                    in_=scales[g0:g1, 4 * q : 4 * q + 4, :].rearrange("g r n -> r g n").bitcast(I32),
+                )
+
+        def by_pass(runs):
+            table = []
+            for g0, g1, codes, planes in runs:
+                for g in range(g0, g1):
+                    table.append((codes, planes, g - g0))
+            return table
+
+        def x_src(tb):
+            return (x_words[:, :, 1024 * tb : 1024 * (tb + 1)], x_scales[:, :, 512 * tb : 512 * (tb + 1)])
+
+        def w_src(n):
+            if n < 4:
+                return (Wq_words[:, :, 1024 * n : 1024 * (n + 1)], Wq_scales[:, :, 512 * n : 512 * (n + 1)])
+            return (Wk_words, Wk_scales)
+
+        xop = {}
+        wop = {}
+
+        head_runs = [(0, 3), (3, 8)]
+        xr = [make_run("x0r%d" % j, g0, g1) for j, (g0, g1) in enumerate(head_runs)]
+        wr = [make_run("w0r%d" % j, g0, g1) for j, (g0, g1) in enumerate(head_runs)]
+        for j in range(len(head_runs)):
+            load_codes(xr[j], x_src(0)[0])
+            load_codes(wr[j], w_src(0)[0])
+            load_scales(xr[j], x_src(0)[1])
+            load_scales(wr[j], w_src(0)[1])
+        xop[0] = by_pass(xr)
+        wop[0] = by_pass(wr)
+
+        eps = keep.tile([P, 1], F32, name="eps", tag="eps")
+        nc.vector.memset(eps[:], EPS)
+        warm = keep.tile([P, 1], F32, name="warm", tag="warm")
+        nc.scalar.activation(out=warm[:], in_=eps[:], func=ACT.Sqrt)
+        ident = keep.tile([P, P], BF16, name="ident", tag="ident")
+        make_identity(nc, ident[:])
+
+        tab_sb = keep.tile([P, 1024], BF16, name="tab_sb", tag="tab_sb")
+        b_sb = keep.tile([P, 2560], BF16, name="b_sb", tag="b_sb")
+        nc.sync.dma_start(
+            out=tab_sb[:, 0:256].rearrange("p (t j) -> p t j", t=4), in_=cos.rearrange("(t p) j -> p t j", p=P)
+        )
+        nc.sync.dma_start(
+            out=tab_sb[:, 768:1024].rearrange("p (t j) -> p t j", t=4), in_=sin.rearrange("(t p) j -> p t j", p=P)
+        )
+        nc.sync.dma_start(out=tab_sb[:, 512:640], in_=qn_w.partition_broadcast(P))
+        nc.sync.dma_start(out=tab_sb[:, 640:768], in_=kn_w.partition_broadcast(P))
+        nc.sync.dma_start(out=b_sb[:, 0:2048], in_=bq.partition_broadcast(P))
+        nc.sync.dma_start(out=b_sb[:, 2048:2560], in_=bk.partition_broadcast(P))
+
+        for n in range(1, BANKS):
+            run = make_run("w%d" % n, 0, PASSES)
+            load_scales(run, w_src(n)[1])
+            load_codes(run, w_src(n)[0])
+            wop[n] = by_pass([run])
+        for tb in range(1, BLOCKS):
+            run = make_run("x%d" % tb, 0, PASSES)
+            load_scales(run, x_src(tb)[1])
+            load_codes(run, x_src(tb)[0])
+            xop[tb] = by_pass([run])
+
+        nc.vector.tensor_scalar_mul(out=tab_sb[:, 256:512], in0=tab_sb[:, 768:1024], scalar1=-1.0)
+
+        tabp = tab_pool.tile([P, 1024], BF16, name="tabp", tag="tabp")
+
+        def mx_pass(acc, tb, i, n, g):
+            xc, xs, gx = xop[tb][g]
+            wc, ws, gw = wop[n][g]
+            nc.tensor.matmul_mx(
+                out=acc[:],
+                lhsT=xc[:, gx, 256 * i : 256 * (i + 1)].bitcast(FP4X4),
+                lhsT_scale=xs[:, gx, 128 * i : 128 * (i + 1)],
+                rhs=wc[:, gw, :].bitcast(FP4X4),
+                rhs_scale=ws[:, gw, :],
+                start=(g == 0),
+                stop=(g == PASSES - 1),
+            )
+
+        pairs = [(tb, n, q) for tb in range(BLOCKS) for n in range(BANKS) for q in range(2)]
+        K = len(pairs)
+        accs = {}
+        v2s = {}
+        abs_ = {}
+        r2s = {}
+        sss = {}
+        rmss = {}
+        rstds = {}
+        y2s = {}
+
+        def new_acc():
+            acc = acc_pool.tile([P, 512], F32, name="acc", tag="acc")
+            return acc
+
+        def emit_mx(k):
+            if k in accs:
+                return
+            tb, n, q = pairs[k]
+            if k == 0:
+                accs[0] = [new_acc(), new_acc()]
+                accs[1] = [new_acc(), new_acc()]
+                for g in range(PASSES):
+                    for i in range(4):
+                        mx_pass(accs[i // 2][i % 2], 0, i, 0, g)
+                nc.tensor.matmul(out=tabp[:, 0:512], lhsT=ident[:], rhs=tab_sb[:, 0:512], start=True, stop=True)
+                nc.tensor.matmul(out=tabp[:, 512:1024], lhsT=ident[:], rhs=tab_sb[:, 512:1024], start=True, stop=True)
+                return
+            accs[k] = [new_acc(), new_acc()]
+            for u in range(2):
+                for g in range(PASSES):
+                    mx_pass(accs[k][u], tb, 2 * q + u, n, g)
+
+        def alloc(k):
+            v2s[k] = work.tile([P, 2, 512], F32, name="v2", tag="v2", bufs=3)
+            abs_[k] = work.tile([P, 2, 2, 512], F32, name="ab", tag="ab", bufs=3)
+            r2s[k] = work.tile([P, 2, 512], F32, name="r2", tag="r2", bufs=3)
+            sss[k] = work.tile([P, 8], F32, name="ss", tag="ss", bufs=3)
+            rmss[k] = work.tile([P, 8], F32, name="rms", tag="rms", bufs=3)
+            rstds[k] = work.tile([P, 8], F32, name="rstd", tag="rstd", bufs=3)
+            y2s[k] = work.tile([P, 2, 512], F32, name="y2", tag="y2", bufs=3)
+
+        def p1(k, u):
+            tb, n, q = pairs[k]
+            nc.vector.tensor_tensor(
+                out=v2s[k][:, u, :].rearrange("p (h e j) -> p h e j", h=4, e=2),
+                in0=accs[k][u][:].rearrange("p (h j e) -> p h e j", h=4, e=2),
+                in1=b_sb[:, 512 * n : 512 * (n + 1)].rearrange("p (h j e) -> p h e j", h=4, e=2),
+                op=ALU.add,
+            )
+
+        def halves(t3):
+            return t3.rearrange("p u (h f j) -> p u h f j", h=4, f=2)
+
+        def table(src, col, k, u0, nu, reps):
+            q = pairs[k][2]
+            t0 = 2 * q + u0
+            return (
+                src[:, col : col + 256]
+                .rearrange("p (t j) -> p t j", t=4)[:, t0 : t0 + nu, :]
+                .unsqueeze(2)
+                .to_broadcast([P, nu, reps, 64])
+            )
+
+        def a(k, u0, nu):
+            nc.vector.tensor_tensor(
+                out=abs_[k][:, 0, u0 : u0 + nu, :].rearrange("p u (m j) -> p u m j", j=64),
+                in0=v2s[k][:, u0 : u0 + nu, :].rearrange("p u (m j) -> p u m j", j=64),
+                in1=table(tabp, 0, k, u0, nu, 8),
+                op=ALU.mult,
+            )
+
+        def b0(k, u0, nu):
+            nc.vector.tensor_tensor(
+                out=halves(abs_[k][:, 1, u0 : u0 + nu, :])[:, :, :, 0, :],
+                in0=halves(v2s[k][:, u0 : u0 + nu, :])[:, :, :, 1, :],
+                in1=table(tabp, 256, k, u0, nu, 4),
+                op=ALU.mult,
+            )
+
+        def b1(k, u0, nu, on_vector=False):
+            eng = nc.vector if on_vector else nc.gpsimd
+            eng.tensor_tensor(
+                out=halves(abs_[k][:, 1, u0 : u0 + nu, :])[:, :, :, 1, :],
+                in0=halves(v2s[k][:, u0 : u0 + nu, :])[:, :, :, 0, :],
+                in1=table(tabp if on_vector else tab_sb, 768, k, u0, nu, 4),
+                op=ALU.mult,
+            )
+
+        def plus(k, u0, nu, on_vector=False):
+            eng = nc.vector if on_vector else nc.gpsimd
+            eng.tensor_tensor(
+                out=r2s[k][:, u0 : u0 + nu, :],
+                in0=abs_[k][:, 0, u0 : u0 + nu, :],
+                in1=abs_[k][:, 1, u0 : u0 + nu, :],
+                op=ALU.add,
+            )
+
+        def squares(k, u0, nu):
+            for u in range(u0, u0 + nu):
+                for h in range(4):
+                    junk = work.tile([P, 2, 128], BF16, name="junk", tag="junk", bufs=4)
+                    nc.scalar.activation(
+                        out=junk[:],
+                        in_=abs_[k][:, :, u, 128 * h : 128 * (h + 1)],
+                        func=ACT.Square,
+                        accum_out=sss[k][:, 4 * u + h : 4 * u + h + 1],
+                    )
+            cols = slice(4 * u0, 4 * (u0 + nu))
+            nc.scalar.activation(
+                out=rmss[k][:, cols], in_=sss[k][:, cols], func=ACT.Sqrt, scale=1.0 / 128.0, bias=eps[:, 0:1]
+            )
+
+        def recip(k, u0, nu):
+            cols = slice(4 * u0, 4 * (u0 + nu))
+            nc.vector.reciprocal(out=rstds[k][:, cols], in_=rmss[k][:, cols])
+
+        def final(k, u0, nu):
+            tb, n, q = pairs[k]
+            wofs = 512 if n < 4 else 640
+            for u in range(u0, u0 + nu):
+                for h in range(4):
+                    nc.vector.scalar_tensor_tensor(
+                        out=y2s[k][:, u, 128 * h : 128 * (h + 1)],
+                        in0=r2s[k][:, u, 128 * h : 128 * (h + 1)],
+                        scalar=rstds[k][:, 4 * u + h : 4 * u + h + 1],
+                        in1=tabp[:, wofs : wofs + 128],
+                        op0=ALU.mult,
+                        op1=ALU.mult,
+                    )
+            r0 = 512 * tb + 256 * q + 128 * u0
+            if n < 4:
+                dst = q_rows[r0 : r0 + 128 * nu, 512 * n : 512 * (n + 1)]
+            else:
+                dst = k_rows[r0 : r0 + 128 * nu, :]
+            nc.sync.dma_start(out=dst.rearrange("(u p) c -> p u c", p=P), in_=y2s[k][:, u0 : u0 + nu, :])
+
+        for c in range(K - 1):
+            emit_mx(c)
+            alloc(c)
+            p1(c, 0)
+            p1(c, 1)
+            b1(c, 0, 2)
+            a(c, 0, 1)
+            a(c, 1, 1)
+            if c >= 1:
+                recip(c - 1, 0, 2)
+            b0(c, 0, 2)
+            squares(c, 0, 2)
+            plus(c, 0, 2)
+            if c >= 1:
+                final(c - 1, 0, 2)
+
+        c = K - 1
+        emit_mx(c)
+        alloc(c)
+        p1(c, 0)
+        b1(c, 0, 1)
+        a(c, 0, 1)
+        b0(c, 0, 1)
+        squares(c, 0, 1)
+        plus(c, 0, 1)
+        p1(c, 1)
+        recip(c - 1, 0, 2)
+        a(c, 1, 1)
+        b0(c, 1, 1)
+        b1(c, 1, 1, on_vector=True)
+        squares(c, 1, 1)
+        final(c - 1, 0, 2)
+        recip(c, 0, 1)
+        plus(c, 1, 1, on_vector=True)
+        recip(c, 1, 1)
+        final(c, 0, 1)
+        final(c, 1, 1)

@@ -73,8 +73,11 @@ def tile_gqaselfattention_pa_kernel(
         wop = {}
 
         head_runs = [(0, 3), (3, 8)]
-        xr = [make_run("x0r%d" % j, g0, g1) for j, (g0, g1) in enumerate(head_runs)]
-        wr = [make_run("w0r%d" % j, g0, g1) for j, (g0, g1) in enumerate(head_runs)]
+        xr = []
+        wr = []
+        for j, (g0, g1) in enumerate(head_runs):
+            xr.append(make_run("x0r%d" % j, g0, g1))
+            wr.append(make_run("w0r%d" % j, g0, g1))
         for j in range(len(head_runs)):
             load_codes(xr[j], x_src(0)[0])
             load_codes(wr[j], w_src(0)[0])
@@ -91,7 +94,19 @@ def tile_gqaselfattention_pa_kernel(
         make_identity(nc, ident[:])
 
         tab_sb = keep.tile([P, 1024], BF16, name="tab_sb", tag="tab_sb")
-        b_sb = keep.tile([P, 2560], BF16, name="b_sb", tag="b_sb")
+        b_sb = [keep.tile([P, 512], BF16, name="b%d" % n, tag="b%d" % n) for n in range(BANKS)]
+
+        def load_bias(n):
+            src = bq[512 * n : 512 * (n + 1)] if n < 4 else bk
+            nc.sync.dma_start(out=b_sb[n][:], in_=src.partition_broadcast(P))
+
+        def load_w(n):
+            run = make_run("w%d" % n, 0, PASSES)
+            load_scales(run, w_src(n)[1])
+            load_codes(run, w_src(n)[0])
+            wop[n] = by_pass([run])
+
+        load_w(1)
         nc.sync.dma_start(
             out=tab_sb[:, 0:256].rearrange("p (t j) -> p t j", t=4), in_=cos.rearrange("(t p) j -> p t j", p=P)
         )
@@ -100,14 +115,11 @@ def tile_gqaselfattention_pa_kernel(
         )
         nc.sync.dma_start(out=tab_sb[:, 512:640], in_=qn_w.partition_broadcast(P))
         nc.sync.dma_start(out=tab_sb[:, 640:768], in_=kn_w.partition_broadcast(P))
-        nc.sync.dma_start(out=b_sb[:, 0:2048], in_=bq.partition_broadcast(P))
-        nc.sync.dma_start(out=b_sb[:, 2048:2560], in_=bk.partition_broadcast(P))
-
-        for n in range(1, BANKS):
-            run = make_run("w%d" % n, 0, PASSES)
-            load_scales(run, w_src(n)[1])
-            load_codes(run, w_src(n)[0])
-            wop[n] = by_pass([run])
+        load_bias(0)
+        for n in range(2, BANKS):
+            load_bias(n - 1)
+            load_w(n)
+        load_bias(BANKS - 1)
         for tb in range(1, BLOCKS):
             run = make_run("x%d" % tb, 0, PASSES)
             load_scales(run, x_src(tb)[1])
@@ -141,6 +153,7 @@ def tile_gqaselfattention_pa_kernel(
         rmss = {}
         rstds = {}
         y2s = {}
+        rws = {}
 
         def new_acc():
             acc = acc_pool.tile([P, 512], F32, name="acc", tag="acc")
@@ -172,13 +185,14 @@ def tile_gqaselfattention_pa_kernel(
             rmss[k] = work.tile([P, 8], F32, name="rms", tag="rms", bufs=3)
             rstds[k] = work.tile([P, 8], F32, name="rstd", tag="rstd", bufs=3)
             y2s[k] = work.tile([P, 2, 512], F32, name="y2", tag="y2", bufs=3)
+            rws[k] = work.tile([P, 2, 512], F32, name="rw", tag="rw", bufs=3)
 
         def p1(k, u):
             tb, n, q = pairs[k]
             nc.vector.tensor_tensor(
                 out=v2s[k][:, u, :].rearrange("p (h e j) -> p h e j", h=4, e=2),
                 in0=accs[k][u][:].rearrange("p (h j e) -> p h e j", h=4, e=2),
-                in1=b_sb[:, 512 * n : 512 * (n + 1)].rearrange("p (h j e) -> p h e j", h=4, e=2),
+                in1=b_sb[n][:].rearrange("p (h j e) -> p h e j", h=4, e=2),
                 op=ALU.add,
             )
 
@@ -229,13 +243,14 @@ def tile_gqaselfattention_pa_kernel(
                 op=ALU.add,
             )
 
-        def squares(k, u0, nu):
+        def squares(k, u0, nu, of_sum=True):
             for u in range(u0, u0 + nu):
                 for h in range(4):
                     junk = work.tile([P, 2, 128], BF16, name="junk", tag="junk", bufs=4)
+                    cols = slice(128 * h, 128 * (h + 1))
                     nc.scalar.activation(
-                        out=junk[:],
-                        in_=abs_[k][:, :, u, 128 * h : 128 * (h + 1)],
+                        out=junk[:, 0, :] if of_sum else junk[:],
+                        in_=r2s[k][:, u, cols] if of_sum else abs_[k][:, :, u, cols],
                         func=ACT.Square,
                         accum_out=sss[k][:, 4 * u + h : 4 * u + h + 1],
                     )
@@ -248,19 +263,37 @@ def tile_gqaselfattention_pa_kernel(
             cols = slice(4 * u0, 4 * (u0 + nu))
             nc.vector.reciprocal(out=rstds[k][:, cols], in_=rmss[k][:, cols])
 
-        def final(k, u0, nu):
+        def gain(k, u0, nu):
+            wofs = 512 if pairs[k][1] < 4 else 640
+            nc.vector.tensor_tensor(
+                out=rws[k][:, u0 : u0 + nu, :].rearrange("p u (h d) -> p (u h) d", d=128),
+                in0=r2s[k][:, u0 : u0 + nu, :].rearrange("p u (h d) -> p (u h) d", d=128),
+                in1=tabp[:, wofs : wofs + 128].unsqueeze(1).to_broadcast([P, 4 * nu, 128]),
+                op=ALU.mult,
+            )
+
+        def final(k, u0, nu, on_vector=False):
             tb, n, q = pairs[k]
             wofs = 512 if n < 4 else 640
             for u in range(u0, u0 + nu):
                 for h in range(4):
-                    nc.vector.scalar_tensor_tensor(
-                        out=y2s[k][:, u, 128 * h : 128 * (h + 1)],
-                        in0=r2s[k][:, u, 128 * h : 128 * (h + 1)],
-                        scalar=rstds[k][:, 4 * u + h : 4 * u + h + 1],
-                        in1=tabp[:, wofs : wofs + 128],
-                        op0=ALU.mult,
-                        op1=ALU.mult,
-                    )
+                    cols = slice(128 * h, 128 * (h + 1))
+                    if on_vector:
+                        nc.vector.scalar_tensor_tensor(
+                            out=y2s[k][:, u, cols],
+                            in0=r2s[k][:, u, cols],
+                            scalar=rstds[k][:, 4 * u + h : 4 * u + h + 1],
+                            in1=tabp[:, wofs : wofs + 128],
+                            op0=ALU.mult,
+                            op1=ALU.mult,
+                        )
+                    else:
+                        nc.scalar.activation(
+                            out=y2s[k][:, u, cols],
+                            in_=rws[k][:, u, cols],
+                            func=ACT.Copy,
+                            scale=rstds[k][:, 4 * u + h : 4 * u + h + 1],
+                        )
             r0 = 512 * tb + 256 * q + 128 * u0
             if n < 4:
                 dst = q_rows[r0 : r0 + 128 * nu, 512 * n : 512 * (n + 1)]
@@ -276,13 +309,15 @@ def tile_gqaselfattention_pa_kernel(
             b1(c, 0, 2)
             a(c, 0, 1)
             a(c, 1, 1)
-            if c >= 1:
-                recip(c - 1, 0, 2)
             b0(c, 0, 2)
-            squares(c, 0, 2)
             plus(c, 0, 2)
             if c >= 1:
-                final(c - 1, 0, 2)
+                squares(c - 1, 0, 2)
+            if c >= 2:
+                final(c - 2, 0, 2)
+            if c >= 1:
+                recip(c - 1, 0, 2)
+                gain(c - 1, 0, 2)
 
         c = K - 1
         emit_mx(c)
@@ -291,17 +326,18 @@ def tile_gqaselfattention_pa_kernel(
         b1(c, 0, 1)
         a(c, 0, 1)
         b0(c, 0, 1)
-        squares(c, 0, 1)
         plus(c, 0, 1)
+        final(c - 2, 0, 2)
+        squares(c - 1, 0, 2)
         p1(c, 1)
-        recip(c - 1, 0, 2)
         a(c, 1, 1)
         b0(c, 1, 1)
         b1(c, 1, 1, on_vector=True)
-        squares(c, 1, 1)
-        final(c - 1, 0, 2)
-        recip(c, 0, 1)
+        squares(c, 0, 1)
+        squares(c, 1, 1, of_sum=False)
+        recip(c - 1, 0, 2)
         plus(c, 1, 1, on_vector=True)
-        recip(c, 1, 1)
-        final(c, 0, 1)
-        final(c, 1, 1)
+        final(c - 1, 0, 2, on_vector=True)
+        recip(c, 0, 2)
+        final(c, 0, 1, on_vector=True)
+        final(c, 1, 1, on_vector=True)

@@ -73,11 +73,8 @@ def tile_gqaselfattention_pa_kernel(
         wop = {}
 
         head_runs = [(0, 3), (3, 8)]
-        xr = []
-        wr = []
-        for j, (g0, g1) in enumerate(head_runs):
-            xr.append(make_run("x0r%d" % j, g0, g1))
-            wr.append(make_run("w0r%d" % j, g0, g1))
+        xr = [make_run("x0r%d" % j, g0, g1) for j, (g0, g1) in enumerate(head_runs)]
+        wr = [make_run("w0r%d" % j, g0, g1) for j, (g0, g1) in enumerate(head_runs)]
         for j in range(len(head_runs)):
             load_codes(xr[j], x_src(0)[0])
             load_codes(wr[j], w_src(0)[0])
@@ -94,19 +91,7 @@ def tile_gqaselfattention_pa_kernel(
         make_identity(nc, ident[:])
 
         tab_sb = keep.tile([P, 1024], BF16, name="tab_sb", tag="tab_sb")
-        b_sb = [keep.tile([P, 512], BF16, name="b%d" % n, tag="b%d" % n) for n in range(BANKS)]
-
-        def load_bias(n):
-            src = bq[512 * n : 512 * (n + 1)] if n < 4 else bk
-            nc.sync.dma_start(out=b_sb[n][:], in_=src.partition_broadcast(P))
-
-        def load_w(n):
-            run = make_run("w%d" % n, 0, PASSES)
-            load_scales(run, w_src(n)[1])
-            load_codes(run, w_src(n)[0])
-            wop[n] = by_pass([run])
-
-        load_w(1)
+        b_sb = keep.tile([P, 2560], BF16, name="b_sb", tag="b_sb")
         nc.sync.dma_start(
             out=tab_sb[:, 0:256].rearrange("p (t j) -> p t j", t=4), in_=cos.rearrange("(t p) j -> p t j", p=P)
         )
@@ -115,11 +100,14 @@ def tile_gqaselfattention_pa_kernel(
         )
         nc.sync.dma_start(out=tab_sb[:, 512:640], in_=qn_w.partition_broadcast(P))
         nc.sync.dma_start(out=tab_sb[:, 640:768], in_=kn_w.partition_broadcast(P))
-        load_bias(0)
-        for n in range(2, BANKS):
-            load_bias(n - 1)
-            load_w(n)
-        load_bias(BANKS - 1)
+        nc.sync.dma_start(out=b_sb[:, 0:2048], in_=bq.partition_broadcast(P))
+        nc.sync.dma_start(out=b_sb[:, 2048:2560], in_=bk.partition_broadcast(P))
+
+        for n in range(1, BANKS):
+            run = make_run("w%d" % n, 0, PASSES)
+            load_scales(run, w_src(n)[1])
+            load_codes(run, w_src(n)[0])
+            wop[n] = by_pass([run])
         for tb in range(1, BLOCKS):
             run = make_run("x%d" % tb, 0, PASSES)
             load_scales(run, x_src(tb)[1])
@@ -153,7 +141,6 @@ def tile_gqaselfattention_pa_kernel(
         rmss = {}
         rstds = {}
         y2s = {}
-        rws = {}
 
         def new_acc():
             acc = acc_pool.tile([P, 512], F32, name="acc", tag="acc")
@@ -180,19 +167,18 @@ def tile_gqaselfattention_pa_kernel(
         def alloc(k):
             v2s[k] = work.tile([P, 2, 512], F32, name="v2", tag="v2", bufs=3)
             abs_[k] = work.tile([P, 2, 2, 512], F32, name="ab", tag="ab", bufs=3)
-            r2s[k] = work.tile([P, 2, 512], F32, name="r2", tag="r2", bufs=3)
-            sss[k] = work.tile([P, 8], F32, name="ss", tag="ss", bufs=3)
-            rmss[k] = work.tile([P, 8], F32, name="rms", tag="rms", bufs=3)
-            rstds[k] = work.tile([P, 8], F32, name="rstd", tag="rstd", bufs=3)
+            r2s[k] = work.tile([P, 2, 512], F32, name="r2", tag="r2", bufs=4)
+            sss[k] = work.tile([P, 8], F32, name="ss", tag="ss", bufs=4)
+            rmss[k] = work.tile([P, 8], F32, name="rms", tag="rms", bufs=4)
+            rstds[k] = work.tile([P, 8], F32, name="rstd", tag="rstd", bufs=4)
             y2s[k] = work.tile([P, 2, 512], F32, name="y2", tag="y2", bufs=3)
-            rws[k] = work.tile([P, 2, 512], F32, name="rw", tag="rw", bufs=3)
 
         def p1(k, u):
             tb, n, q = pairs[k]
             nc.vector.tensor_tensor(
                 out=v2s[k][:, u, :].rearrange("p (h e j) -> p h e j", h=4, e=2),
                 in0=accs[k][u][:].rearrange("p (h j e) -> p h e j", h=4, e=2),
-                in1=b_sb[n][:].rearrange("p (h j e) -> p h e j", h=4, e=2),
+                in1=b_sb[:, 512 * n : 512 * (n + 1)].rearrange("p (h j e) -> p h e j", h=4, e=2),
                 op=ALU.add,
             )
 
@@ -243,14 +229,13 @@ def tile_gqaselfattention_pa_kernel(
                 op=ALU.add,
             )
 
-        def squares(k, u0, nu, of_sum=True):
+        def squares(k, u0, nu):
             for u in range(u0, u0 + nu):
                 for h in range(4):
                     junk = work.tile([P, 2, 128], BF16, name="junk", tag="junk", bufs=4)
-                    cols = slice(128 * h, 128 * (h + 1))
                     nc.scalar.activation(
-                        out=junk[:, 0, :] if of_sum else junk[:],
-                        in_=r2s[k][:, u, cols] if of_sum else abs_[k][:, :, u, cols],
+                        out=junk[:],
+                        in_=abs_[k][:, :, u, 128 * h : 128 * (h + 1)],
                         func=ACT.Square,
                         accum_out=sss[k][:, 4 * u + h : 4 * u + h + 1],
                     )
@@ -263,37 +248,19 @@ def tile_gqaselfattention_pa_kernel(
             cols = slice(4 * u0, 4 * (u0 + nu))
             nc.vector.reciprocal(out=rstds[k][:, cols], in_=rmss[k][:, cols])
 
-        def gain(k, u0, nu):
+        def final_head(k, m):
             wofs = 512 if pairs[k][1] < 4 else 640
-            nc.vector.tensor_tensor(
-                out=rws[k][:, u0 : u0 + nu, :].rearrange("p u (h d) -> p (u h) d", d=128),
-                in0=r2s[k][:, u0 : u0 + nu, :].rearrange("p u (h d) -> p (u h) d", d=128),
-                in1=tabp[:, wofs : wofs + 128].unsqueeze(1).to_broadcast([P, 4 * nu, 128]),
-                op=ALU.mult,
+            nc.vector.scalar_tensor_tensor(
+                out=y2s[k][:, m // 4, 128 * (m % 4) : 128 * (m % 4 + 1)],
+                in0=r2s[k][:, m // 4, 128 * (m % 4) : 128 * (m % 4 + 1)],
+                scalar=rstds[k][:, m : m + 1],
+                in1=tabp[:, wofs : wofs + 128],
+                op0=ALU.mult,
+                op1=ALU.mult,
             )
 
-        def final(k, u0, nu, on_vector=False):
+        def store(k, u0, nu):
             tb, n, q = pairs[k]
-            wofs = 512 if n < 4 else 640
-            for u in range(u0, u0 + nu):
-                for h in range(4):
-                    cols = slice(128 * h, 128 * (h + 1))
-                    if on_vector:
-                        nc.vector.scalar_tensor_tensor(
-                            out=y2s[k][:, u, cols],
-                            in0=r2s[k][:, u, cols],
-                            scalar=rstds[k][:, 4 * u + h : 4 * u + h + 1],
-                            in1=tabp[:, wofs : wofs + 128],
-                            op0=ALU.mult,
-                            op1=ALU.mult,
-                        )
-                    else:
-                        nc.scalar.activation(
-                            out=y2s[k][:, u, cols],
-                            in_=rws[k][:, u, cols],
-                            func=ACT.Copy,
-                            scale=rstds[k][:, 4 * u + h : 4 * u + h + 1],
-                        )
             r0 = 512 * tb + 256 * q + 128 * u0
             if n < 4:
                 dst = q_rows[r0 : r0 + 128 * nu, 512 * n : 512 * (n + 1)]
@@ -301,7 +268,18 @@ def tile_gqaselfattention_pa_kernel(
                 dst = k_rows[r0 : r0 + 128 * nu, :]
             nc.sync.dma_start(out=dst.rearrange("(u p) c -> p u c", p=P), in_=y2s[k][:, u0 : u0 + nu, :])
 
+        def final(k, u0, nu):
+            for m in range(4 * u0, 4 * (u0 + nu)):
+                final_head(k, m)
+            store(k, u0, nu)
+
+        queue = [(k, m) for k in range(K - 2) for m in range(8)]
+        done = 0
+        inverted = set()
         for c in range(K - 1):
+            quota = 0 if c < 2 else (8 if c < K - 5 else 10)
+            todo = queue[done : done + quota]
+            done += quota
             emit_mx(c)
             alloc(c)
             p1(c, 0)
@@ -309,15 +287,19 @@ def tile_gqaselfattention_pa_kernel(
             b1(c, 0, 2)
             a(c, 0, 1)
             a(c, 1, 1)
+            if todo and todo[0][0] not in inverted:
+                recip(todo[0][0], 0, 2)
+                inverted.add(todo[0][0])
             b0(c, 0, 2)
+            squares(c, 0, 2)
             plus(c, 0, 2)
-            if c >= 1:
-                squares(c - 1, 0, 2)
-            if c >= 2:
-                final(c - 2, 0, 2)
-            if c >= 1:
-                recip(c - 1, 0, 2)
-                gain(c - 1, 0, 2)
+            if todo and todo[-1][0] not in inverted:
+                recip(todo[-1][0], 0, 2)
+                inverted.add(todo[-1][0])
+            for k, m in todo:
+                final_head(k, m)
+                if m == 7:
+                    store(k, 0, 2)
 
         c = K - 1
         emit_mx(c)
@@ -326,18 +308,17 @@ def tile_gqaselfattention_pa_kernel(
         b1(c, 0, 1)
         a(c, 0, 1)
         b0(c, 0, 1)
+        squares(c, 0, 1)
         plus(c, 0, 1)
-        final(c - 2, 0, 2)
-        squares(c - 1, 0, 2)
         p1(c, 1)
+        recip(c - 1, 0, 2)
         a(c, 1, 1)
         b0(c, 1, 1)
         b1(c, 1, 1, on_vector=True)
-        squares(c, 0, 1)
-        squares(c, 1, 1, of_sum=False)
-        recip(c - 1, 0, 2)
+        squares(c, 1, 1)
+        final(c - 1, 0, 2)
+        recip(c, 0, 1)
         plus(c, 1, 1, on_vector=True)
-        final(c - 1, 0, 2, on_vector=True)
-        recip(c, 0, 2)
-        final(c, 0, 1, on_vector=True)
-        final(c, 1, 1, on_vector=True)
+        recip(c, 1, 1)
+        final(c, 0, 1)
+        final(c, 1, 1)

@@ -141,6 +141,8 @@ def tile_gqaselfattention_pa_kernel(
         rmss = {}
         rstds = {}
         y2s = {}
+        rws = {}
+        KS = K - 8
 
         def new_acc():
             acc = acc_pool.tile([P, 512], F32, name="acc", tag="acc")
@@ -172,6 +174,8 @@ def tile_gqaselfattention_pa_kernel(
             rmss[k] = work.tile([P, 8], F32, name="rms", tag="rms", bufs=4)
             rstds[k] = work.tile([P, 8], F32, name="rstd", tag="rstd", bufs=4)
             y2s[k] = work.tile([P, 2, 512], F32, name="y2", tag="y2", bufs=3)
+            if k < KS:
+                rws[k] = work.tile([P, 2, 512], F32, name="rw", tag="rw", bufs=3)
 
         def p1(k, u):
             tb, n, q = pairs[k]
@@ -229,13 +233,14 @@ def tile_gqaselfattention_pa_kernel(
                 op=ALU.add,
             )
 
-        def squares(k, u0, nu):
+        def squares(k, u0, nu, of_sum=False):
             for u in range(u0, u0 + nu):
                 for h in range(4):
                     junk = work.tile([P, 2, 128], BF16, name="junk", tag="junk", bufs=4)
+                    hd = slice(128 * h, 128 * (h + 1))
                     nc.scalar.activation(
-                        out=junk[:],
-                        in_=abs_[k][:, :, u, 128 * h : 128 * (h + 1)],
+                        out=junk[:, 0, :] if of_sum else junk[:],
+                        in_=r2s[k][:, u, hd] if of_sum else abs_[k][:, :, u, hd],
                         func=ACT.Square,
                         accum_out=sss[k][:, 4 * u + h : 4 * u + h + 1],
                     )
@@ -259,6 +264,22 @@ def tile_gqaselfattention_pa_kernel(
                 op1=ALU.mult,
             )
 
+        def gain(k):
+            wofs = 512 if pairs[k][1] < 4 else 640
+            nc.vector.tensor_tensor(
+                out=rws[k][:].rearrange("p u (h d) -> p (u h) d", d=128),
+                in0=r2s[k][:].rearrange("p u (h d) -> p (u h) d", d=128),
+                in1=tabp[:, wofs : wofs + 128].unsqueeze(1).to_broadcast([P, 8, 128]),
+                op=ALU.mult,
+            )
+
+        def scale_rows(k):
+            for m in range(8):
+                hd = slice(128 * (m % 4), 128 * (m % 4 + 1))
+                nc.scalar.activation(
+                    out=y2s[k][:, m // 4, hd], in_=rws[k][:, m // 4, hd], func=ACT.Copy, scale=rstds[k][:, m : m + 1]
+                )
+
         def store(k, u0, nu):
             tb, n, q = pairs[k]
             r0 = 512 * tb + 256 * q + 128 * u0
@@ -273,25 +294,37 @@ def tile_gqaselfattention_pa_kernel(
                 final_head(k, m)
             store(k, u0, nu)
 
-        queue = [(k, m) for k in range(K - 2) for m in range(8)]
+        queue = [(k, m) for k in range(KS, K - 2) for m in range(8)]
         done = 0
         inverted = set()
         for c in range(K - 1):
-            quota = 0 if c < 2 else (8 if c < K - 5 else 10)
+            quota = 0 if c < KS + 2 else (8 if c < K - 5 else 10)
             todo = queue[done : done + quota]
             done += quota
+            old = c - 2 if 2 <= c < KS + 2 else None
             emit_mx(c)
             alloc(c)
             p1(c, 0)
             p1(c, 1)
             b1(c, 0, 2)
-            a(c, 0, 1)
-            a(c, 1, 1)
+            if old is not None:
+                recip(old, 0, 2)
+                gain(old)
+                a(c, 0, 2)
+            else:
+                a(c, 0, 1)
+                a(c, 1, 1)
             if todo and todo[0][0] not in inverted:
                 recip(todo[0][0], 0, 2)
                 inverted.add(todo[0][0])
             b0(c, 0, 2)
-            squares(c, 0, 2)
+            if 1 <= c <= KS:
+                squares(c - 1, 0, 2, of_sum=True)
+            if c >= KS:
+                squares(c, 0, 2)
+            if old is not None:
+                scale_rows(old)
+                store(old, 0, 2)
             plus(c, 0, 2)
             if todo and todo[-1][0] not in inverted:
                 recip(todo[-1][0], 0, 2)

@@ -72,14 +72,20 @@ def tile_gqaselfattention_pa_kernel(
         xop = {}
         wop = {}
 
-        head_runs = [(0, 3), (3, 8)]
-        xr = [make_run("x0r%d" % j, g0, g1) for j, (g0, g1) in enumerate(head_runs)]
-        wr = [make_run("w0r%d" % j, g0, g1) for j, (g0, g1) in enumerate(head_runs)]
-        for j in range(len(head_runs)):
-            load_codes(xr[j], x_src(0)[0])
-            load_codes(wr[j], w_src(0)[0])
-            load_scales(xr[j], x_src(0)[1])
-            load_scales(wr[j], w_src(0)[1])
+        head_runs = [(0, 4), (4, 8)]
+        xr = []
+        wr = []
+        for j, (g0, g1) in enumerate(head_runs):
+            xr.append(make_run("x0r%d" % j, g0, g1))
+            wr.append(make_run("w0r%d" % j, g0, g1))
+        load_scales(xr[0], x_src(0)[1])
+        load_codes(xr[0], x_src(0)[0])
+        load_codes(wr[0], w_src(0)[0])
+        load_scales(wr[0], w_src(0)[1])
+        load_codes(xr[1], x_src(0)[0])
+        load_codes(wr[1], w_src(0)[0])
+        load_scales(xr[1], x_src(0)[1])
+        load_scales(wr[1], w_src(0)[1])
         xop[0] = by_pass(xr)
         wop[0] = by_pass(wr)
 
@@ -92,6 +98,25 @@ def tile_gqaselfattention_pa_kernel(
 
         tab_sb = keep.tile([P, 1024], BF16, name="tab_sb", tag="tab_sb")
         b_sb = keep.tile([P, 2560], BF16, name="b_sb", tag="b_sb")
+
+        w_runs = {}
+        for n in range(1, BANKS):
+            w_runs[n] = make_run("w%d" % n, 0, PASSES)
+            wop[n] = by_pass([w_runs[n]])
+        x_runs = {}
+        for tb in range(1, BLOCKS):
+            x_runs[tb] = make_run("x%d" % tb, 0, PASSES)
+            xop[tb] = by_pass([x_runs[tb]])
+
+        def load_w(n):
+            load_scales(w_runs[n], w_src(n)[1])
+            load_codes(w_runs[n], w_src(n)[0])
+
+        def load_x(tb):
+            load_scales(x_runs[tb], x_src(tb)[1])
+            load_codes(x_runs[tb], x_src(tb)[0])
+
+        load_w(1)
         nc.sync.dma_start(
             out=tab_sb[:, 0:256].rearrange("p (t j) -> p t j", t=4), in_=cos.rearrange("(t p) j -> p t j", p=P)
         )
@@ -102,17 +127,9 @@ def tile_gqaselfattention_pa_kernel(
         nc.sync.dma_start(out=tab_sb[:, 640:768], in_=kn_w.partition_broadcast(P))
         nc.sync.dma_start(out=b_sb[:, 0:2048], in_=bq.partition_broadcast(P))
         nc.sync.dma_start(out=b_sb[:, 2048:2560], in_=bk.partition_broadcast(P))
-
-        for n in range(1, BANKS):
-            run = make_run("w%d" % n, 0, PASSES)
-            load_scales(run, w_src(n)[1])
-            load_codes(run, w_src(n)[0])
-            wop[n] = by_pass([run])
-        for tb in range(1, BLOCKS):
-            run = make_run("x%d" % tb, 0, PASSES)
-            load_scales(run, x_src(tb)[1])
-            load_codes(run, x_src(tb)[0])
-            xop[tb] = by_pass([run])
+        for n in range(2, BANKS):
+            load_w(n)
+        load_x(1)
 
         nc.vector.tensor_scalar_mul(out=tab_sb[:, 256:512], in0=tab_sb[:, 768:1024], scalar1=-1.0)
 
@@ -141,8 +158,6 @@ def tile_gqaselfattention_pa_kernel(
         rmss = {}
         rstds = {}
         y2s = {}
-        rws = {}
-        KS = K - 8
 
         def new_acc():
             acc = acc_pool.tile([P, 512], F32, name="acc", tag="acc")
@@ -174,8 +189,6 @@ def tile_gqaselfattention_pa_kernel(
             rmss[k] = work.tile([P, 8], F32, name="rms", tag="rms", bufs=4)
             rstds[k] = work.tile([P, 8], F32, name="rstd", tag="rstd", bufs=4)
             y2s[k] = work.tile([P, 2, 512], F32, name="y2", tag="y2", bufs=3)
-            if k < KS:
-                rws[k] = work.tile([P, 2, 512], F32, name="rw", tag="rw", bufs=3)
 
         def p1(k, u):
             tb, n, q = pairs[k]
@@ -233,14 +246,13 @@ def tile_gqaselfattention_pa_kernel(
                 op=ALU.add,
             )
 
-        def squares(k, u0, nu, of_sum=False):
+        def squares(k, u0, nu):
             for u in range(u0, u0 + nu):
                 for h in range(4):
                     junk = work.tile([P, 2, 128], BF16, name="junk", tag="junk", bufs=4)
-                    hd = slice(128 * h, 128 * (h + 1))
                     nc.scalar.activation(
-                        out=junk[:, 0, :] if of_sum else junk[:],
-                        in_=r2s[k][:, u, hd] if of_sum else abs_[k][:, :, u, hd],
+                        out=junk[:],
+                        in_=abs_[k][:, :, u, 128 * h : 128 * (h + 1)],
                         func=ACT.Square,
                         accum_out=sss[k][:, 4 * u + h : 4 * u + h + 1],
                     )
@@ -264,22 +276,6 @@ def tile_gqaselfattention_pa_kernel(
                 op1=ALU.mult,
             )
 
-        def gain(k):
-            wofs = 512 if pairs[k][1] < 4 else 640
-            nc.vector.tensor_tensor(
-                out=rws[k][:].rearrange("p u (h d) -> p (u h) d", d=128),
-                in0=r2s[k][:].rearrange("p u (h d) -> p (u h) d", d=128),
-                in1=tabp[:, wofs : wofs + 128].unsqueeze(1).to_broadcast([P, 8, 128]),
-                op=ALU.mult,
-            )
-
-        def scale_rows(k):
-            for m in range(8):
-                hd = slice(128 * (m % 4), 128 * (m % 4 + 1))
-                nc.scalar.activation(
-                    out=y2s[k][:, m // 4, hd], in_=rws[k][:, m // 4, hd], func=ACT.Copy, scale=rstds[k][:, m : m + 1]
-                )
-
         def store(k, u0, nu):
             tb, n, q = pairs[k]
             r0 = 512 * tb + 256 * q + 128 * u0
@@ -294,37 +290,25 @@ def tile_gqaselfattention_pa_kernel(
                 final_head(k, m)
             store(k, u0, nu)
 
-        queue = [(k, m) for k in range(KS, K - 2) for m in range(8)]
+        queue = [(k, m) for k in range(K - 2) for m in range(8)]
         done = 0
         inverted = set()
         for c in range(K - 1):
-            quota = 0 if c < KS + 2 else (8 if c < K - 5 else 10)
+            quota = 0 if c < 2 else (8 if c < K - 5 else 10)
             todo = queue[done : done + quota]
             done += quota
-            old = c - 2 if 2 <= c < KS + 2 else None
             emit_mx(c)
             alloc(c)
             p1(c, 0)
             p1(c, 1)
             b1(c, 0, 2)
-            if old is not None:
-                recip(old, 0, 2)
-                gain(old)
-                a(c, 0, 2)
-            else:
-                a(c, 0, 1)
-                a(c, 1, 1)
+            a(c, 0, 1)
+            a(c, 1, 1)
             if todo and todo[0][0] not in inverted:
                 recip(todo[0][0], 0, 2)
                 inverted.add(todo[0][0])
             b0(c, 0, 2)
-            if 1 <= c <= KS:
-                squares(c - 1, 0, 2, of_sum=True)
-            if c >= KS:
-                squares(c, 0, 2)
-            if old is not None:
-                scale_rows(old)
-                store(old, 0, 2)
+            squares(c, 0, 2)
             plus(c, 0, 2)
             if todo and todo[-1][0] not in inverted:
                 recip(todo[-1][0], 0, 2)
@@ -333,6 +317,8 @@ def tile_gqaselfattention_pa_kernel(
                 final_head(k, m)
                 if m == 7:
                     store(k, 0, 2)
+            if c in (4, 8):
+                load_x(c // 4 + 1)
 
         c = K - 1
         emit_mx(c)

@@ -92,7 +92,7 @@ def tile_gqaselfattention_pa_kernel(
         eps = keep.tile([P, 1], F32, name="eps", tag="eps")
         nc.vector.memset(eps[:], EPS)
         warm = keep.tile([P, 1], F32, name="warm", tag="warm")
-        nc.scalar.activation(out=warm[:], in_=eps[:], func=ACT.Sqrt)
+        nc.scalar.activation(out=warm[:], in_=eps[:], func=ACT.Abs_reciprocal_sqrt)
         ident = keep.tile([P, P], BF16, name="ident", tag="ident")
         make_identity(nc, ident[:])
 
@@ -155,7 +155,6 @@ def tile_gqaselfattention_pa_kernel(
         abs_ = {}
         r2s = {}
         sss = {}
-        rmss = {}
         rstds = {}
         y2s = {}
 
@@ -186,7 +185,6 @@ def tile_gqaselfattention_pa_kernel(
             abs_[k] = work.tile([P, 2, 2, 512], F32, name="ab", tag="ab", bufs=3)
             r2s[k] = work.tile([P, 2, 512], F32, name="r2", tag="r2", bufs=4)
             sss[k] = work.tile([P, 8], F32, name="ss", tag="ss", bufs=4)
-            rmss[k] = work.tile([P, 8], F32, name="rms", tag="rms", bufs=4)
             rstds[k] = work.tile([P, 8], F32, name="rstd", tag="rstd", bufs=4)
             y2s[k] = work.tile([P, 2, 512], F32, name="y2", tag="y2", bufs=3)
 
@@ -258,12 +256,15 @@ def tile_gqaselfattention_pa_kernel(
                     )
             cols = slice(4 * u0, 4 * (u0 + nu))
             nc.scalar.activation(
-                out=rmss[k][:, cols], in_=sss[k][:, cols], func=ACT.Sqrt, scale=1.0 / 128.0, bias=eps[:, 0:1]
+                out=rstds[k][:, cols],
+                in_=sss[k][:, cols],
+                func=ACT.Abs_reciprocal_sqrt,
+                scale=1.0 / 128.0,
+                bias=eps[:, 0:1],
             )
 
         def recip(k, u0, nu):
-            cols = slice(4 * u0, 4 * (u0 + nu))
-            nc.vector.reciprocal(out=rstds[k][:, cols], in_=rmss[k][:, cols])
+            return None
 
         def final_head(k, m):
             wofs = 512 if pairs[k][1] < 4 else 640

@@ -263,9 +263,6 @@ def tile_gqaselfattention_pa_kernel(
                 bias=eps[:, 0:1],
             )
 
-        def recip(k, u0, nu):
-            return None
-
         def final_head(k, m):
             wofs = 512 if pairs[k][1] < 4 else 640
             nc.vector.scalar_tensor_tensor(
@@ -286,59 +283,68 @@ def tile_gqaselfattention_pa_kernel(
                 dst = k_rows[r0 : r0 + 128 * nu, :]
             nc.sync.dma_start(out=dst.rearrange("(u p) c -> p u c", p=P), in_=y2s[k][:, u0 : u0 + nu, :])
 
-        def final(k, u0, nu):
-            for m in range(4 * u0, 4 * (u0 + nu)):
-                final_head(k, m)
-            store(k, u0, nu)
+        UNITS = 2 * K
+        FIRST_FINE = K - 3
+        RAMP = UNITS - 8
+        heads = [(k, m) for k in range(K) for m in range(8)]
+        state = {"done": 0}
 
-        queue = [(k, m) for k in range(K - 2) for m in range(8)]
-        done = 0
-        inverted = set()
-        for c in range(K - 1):
-            quota = 0 if c < 2 else (8 if c < K - 5 else 10)
-            todo = queue[done : done + quota]
-            done += quota
-            emit_mx(c)
-            alloc(c)
-            p1(c, 0)
-            p1(c, 1)
-            b1(c, 0, 2)
-            a(c, 0, 1)
-            a(c, 1, 1)
-            if todo and todo[0][0] not in inverted:
-                recip(todo[0][0], 0, 2)
-                inverted.add(todo[0][0])
-            b0(c, 0, 2)
-            squares(c, 0, 2)
-            plus(c, 0, 2)
-            if todo and todo[-1][0] not in inverted:
-                recip(todo[-1][0], 0, 2)
-                inverted.add(todo[-1][0])
-            for k, m in todo:
+        def ready_slot(k, m):
+            if k >= FIRST_FINE:
+                return 2 * k + m // 4 + 3
+            return 2 * k + 3
+
+        def store_head(k, m):
+            tb, n, q = pairs[k]
+            r0 = 512 * tb + 256 * q + 128 * (m // 4)
+            c0 = 128 * (m % 4)
+            if n < 4:
+                dst = q_rows[r0 : r0 + 128, 512 * n + c0 : 512 * n + c0 + 128]
+            else:
+                dst = k_rows[r0 : r0 + 128, c0 : c0 + 128]
+            nc.sync.dma_start(out=dst, in_=y2s[k][:, m // 4, c0 : c0 + 128])
+
+        def finals(slot, quota):
+            for k, m in heads[state["done"] : state["done"] + quota]:
+                assert ready_slot(k, m) <= slot
                 final_head(k, m)
-                if m == 7:
+                if k == K - 1 and m >= 4:
+                    store_head(k, m)
+                elif k >= FIRST_FINE:
+                    if m % 4 == 3:
+                        store(k, m // 4, 1)
+                elif m == 7:
                     store(k, 0, 2)
-            if c in (4, 8):
-                load_x(c // 4 + 1)
+            state["done"] = state["done"] + quota
 
-        c = K - 1
-        emit_mx(c)
-        alloc(c)
-        p1(c, 0)
-        b1(c, 0, 1)
-        a(c, 0, 1)
-        b0(c, 0, 1)
-        squares(c, 0, 1)
-        plus(c, 0, 1)
-        p1(c, 1)
-        recip(c - 1, 0, 2)
-        a(c, 1, 1)
-        b0(c, 1, 1)
-        b1(c, 1, 1, on_vector=True)
-        squares(c, 1, 1)
-        final(c - 1, 0, 2)
-        recip(c, 0, 1)
-        plus(c, 1, 1, on_vector=True)
-        recip(c, 1, 1)
-        final(c, 0, 1)
-        final(c, 1, 1)
+        for n in range(UNITS):
+            c, u = divmod(n, 2)
+            fine = c >= FIRST_FINE
+            if u == 0:
+                emit_mx(c)
+                alloc(c)
+            p1(c, u)
+            if fine:
+                if n < UNITS - 1:
+                    b1(c, u, 1)
+                if n > 2 * FIRST_FINE:
+                    plus((n - 1) // 2, (n - 1) % 2, 1)
+            elif u == 1:
+                b1(c, 0, 2)
+            if n >= 4:
+                finals(n, 2)
+            a(c, u, 1)
+            b0(c, u, 1)
+            if n == UNITS - 1:
+                b1(c, u, 1, on_vector=True)
+            if fine:
+                squares(c, u, 1)
+            elif u == 1:
+                squares(c, 0, 2)
+                plus(c, 0, 2)
+            if n >= 4:
+                finals(n, 3 if RAMP <= n < RAMP + 4 else 2)
+            if u == 1 and c in (4, 8):
+                load_x(c // 4 + 1)
+        plus(K - 1, 1, 1)
+        finals(UNITS + 2, len(heads) - state["done"])

@@ -58,7 +58,7 @@ def tile_gqaselfattention_pa_kernel(
             table = []
             for g0, g1, codes, planes in runs:
                 for g in range(g0, g1):
-                    table.append((codes, planes, g - g0))
+                    table.append((codes, g - g0, planes, g - g0))
             return table
 
         def x_src(tb):
@@ -72,22 +72,27 @@ def tile_gqaselfattention_pa_kernel(
         xop = {}
         wop = {}
 
-        head_runs = [(0, 4), (4, 8)]
-        xr = []
-        wr = []
-        for j, (g0, g1) in enumerate(head_runs):
-            xr.append(make_run("x0r%d" % j, g0, g1))
-            wr.append(make_run("w0r%d" % j, g0, g1))
-        load_scales(xr[0], x_src(0)[1])
-        load_codes(xr[0], x_src(0)[0])
-        load_codes(wr[0], w_src(0)[0])
-        load_scales(wr[0], w_src(0)[1])
-        load_codes(xr[1], x_src(0)[0])
-        load_codes(wr[1], w_src(0)[0])
-        load_scales(xr[1], x_src(0)[1])
-        load_scales(wr[1], w_src(0)[1])
-        xop[0] = by_pass(xr)
-        wop[0] = by_pass(wr)
+        head_runs = [(0, 2), (2, 4), (4, 8)]
+        first = {}
+        for name in ("x0", "w0"):
+            planes = keep.tile([P, PASSES, 512], U8, name=name + "s", tag=name + "s", align_bytes=64)
+            nc.vector.memset(planes[:].bitcast(I32), 0)
+            runs = []
+            for j, (g0, g1) in enumerate(head_runs):
+                codes = keep.tile(
+                    [P, g1 - g0, 1024], U8, name="%sc%d" % (name, j), tag="%sc%d" % (name, j), align_bytes=64
+                )
+                runs.append((g0, g1, codes, planes))
+            first[name] = runs
+        load_codes(first["x0"][0], x_src(0)[0])
+        load_codes(first["w0"][0], w_src(0)[0])
+        load_scales((0, PASSES, None, first["x0"][0][3]), x_src(0)[1])
+        load_scales((0, PASSES, None, first["w0"][0][3]), w_src(0)[1])
+        for j in (1, 2):
+            load_codes(first["x0"][j], x_src(0)[0])
+            load_codes(first["w0"][j], w_src(0)[0])
+        xop[0] = [(codes, g - g0, planes, g) for g0, g1, codes, planes in first["x0"] for g in range(g0, g1)]
+        wop[0] = [(codes, g - g0, planes, g) for g0, g1, codes, planes in first["w0"] for g in range(g0, g1)]
 
         eps = keep.tile([P, 1], F32, name="eps", tag="eps")
         nc.vector.memset(eps[:], EPS)
@@ -136,14 +141,14 @@ def tile_gqaselfattention_pa_kernel(
         tabp = tab_pool.tile([P, 1024], BF16, name="tabp", tag="tabp")
 
         def mx_pass(acc, tb, i, n, g):
-            xc, xs, gx = xop[tb][g]
-            wc, ws, gw = wop[n][g]
+            xc, gx, xs, hx = xop[tb][g]
+            wc, gw, ws, hw = wop[n][g]
             nc.tensor.matmul_mx(
                 out=acc[:],
                 lhsT=xc[:, gx, 256 * i : 256 * (i + 1)].bitcast(FP4X4),
-                lhsT_scale=xs[:, gx, 128 * i : 128 * (i + 1)],
+                lhsT_scale=xs[:, hx, 128 * i : 128 * (i + 1)],
                 rhs=wc[:, gw, :].bitcast(FP4X4),
-                rhs_scale=ws[:, gw, :],
+                rhs_scale=ws[:, hw, :],
                 start=(g == 0),
                 stop=(g == PASSES - 1),
             )

@@ -18,6 +18,7 @@ PASSES = 8
 BLOCKS = 4
 BANKS = 5
 EPS = 1e-6
+WARM = 12
 
 
 def tile_gqaselfattention_pa_kernel(
@@ -71,6 +72,9 @@ def tile_gqaselfattention_pa_kernel(
 
         xop = {}
         wop = {}
+
+        zeros = keep.tile([P, 512], BF16, name="zeros", tag="zeros")
+        nc.gpsimd.memset(zeros[:], 0.0)
 
         head_runs = [(0, 2), (2, 4), (4, 8)]
         first = {}
@@ -139,6 +143,8 @@ def tile_gqaselfattention_pa_kernel(
         nc.vector.tensor_scalar_mul(out=tab_sb[:, 256:512], in0=tab_sb[:, 768:1024], scalar1=-1.0)
 
         tabp = tab_pool.tile([P, 1024], BF16, name="tabp", tag="tabp")
+        for w in range(WARM):
+            nc.tensor.matmul(out=tabp[:, 0:512], lhsT=zeros[:, 0:128], rhs=zeros[:], start=True, stop=True)
 
         def mx_pass(acc, tb, i, n, g):
             xc, gx, xs, hx = xop[tb][g]

@@ -49,7 +49,7 @@ def tile_gqaselfattention_pa_kernel(
 
         def load_scales(run, scales):
             g0, g1, codes, planes = run
-            for q in range(4):
+            for q in (0, 2, 1, 3):
                 nc.sync.dma_start(
                     out=planes[32 * q : 32 * q + 4, :, :].bitcast(I32),
                     in_=scales[g0:g1, 4 * q : 4 * q + 4, :].rearrange("g r n -> r g n").bitcast(I32),

from contextlib import ExitStack

import concourse.mybir as mybir
from concourse.masks import make_identity

FLOPS = 2 * 2048 * 4096 * 2560

F32 = mybir.dt.float32
BF16 = mybir.dt.bfloat16
U8 = mybir.dt.uint8
I32 = mybir.dt.int32
FP4X4 = mybir.dt.float4_e2m1fn_x4
ALU = mybir.AluOpType
ACT = mybir.ActivationFunctionType

P = 128
PASSES = 8
BLOCKS = 4
BANKS = 5
EPS = 1e-6
WARM = 12


def tile_gqaselfattention_pa_kernel(
    tc, x_words, x_scales, Wq_words, Wq_scales, bq, Wk_words, Wk_scales, bk, qn_w, kn_w, cos, sin, out_0, out_1
):
    nc = tc.nc
    q_rows = out_0.rearrange("b t h d -> (b t) (h d)")
    k_rows = out_1.rearrange("b t h d -> (b t) (h d)")

    with ExitStack() as ctx:
        keep = ctx.enter_context(tc.tile_pool(name="keep", bufs=1))
        work = ctx.enter_context(tc.tile_pool(name="work", bufs=2))
        acc_pool = ctx.enter_context(tc.psum_pool(name="acc", bufs=7))
        tab_pool = ctx.enter_context(tc.psum_pool(name="tab", bufs=1))
        ctx.enter_context(tc.manual_schedule())

        def make_run(name, g0, g1):
            codes = keep.tile([P, g1 - g0, 1024], U8, name=name + "c", tag=name + "c", align_bytes=64)
            planes = keep.tile([P, g1 - g0, 512], U8, name=name + "s", tag=name + "s", align_bytes=64)
            nc.vector.memset(planes[:].bitcast(I32), 0)
            return (g0, g1, codes, planes)

        def load_codes(run, words):
            g0, g1, codes, planes = run
            nc.sync.dma_start(
                out=codes[:].bitcast(I32), in_=words[g0:g1].rearrange("g p n -> p g n").bitcast(I32)
            )

        def load_scales(run, scales):
            g0, g1, codes, planes = run
            for q in (0, 2, 1, 3):
                nc.sync.dma_start(
                    out=planes[32 * q : 32 * q + 4, :, :].bitcast(I32),
                    in_=scales[g0:g1, 4 * q : 4 * q + 4, :].rearrange("g r n -> r g n").bitcast(I32),
                )

        def by_pass(runs):
            table = []
            for g0, g1, codes, planes in runs:
                for g in range(g0, g1):
                    table.append((codes, g - g0, planes, g - g0))
            return table

        def x_src(tb):
            return (x_words[:, :, 1024 * tb : 1024 * (tb + 1)], x_scales[:, :, 512 * tb : 512 * (tb + 1)])

        def w_src(n):
            if n < 4:
                return (Wq_words[:, :, 1024 * n : 1024 * (n + 1)], Wq_scales[:, :, 512 * n : 512 * (n + 1)])
            return (Wk_words, Wk_scales)

        xop = {}
        wop = {}

        zeros = keep.tile([P, 512], BF16, name="zeros", tag="zeros")
        nc.gpsimd.memset(zeros[:], 0.0)

        head_runs = [(0, 2), (2, 4), (4, 8)]
        first = {}
        for name in ("x0", "w0"):
            planes = keep.tile([P, PASSES, 512], U8, name=name + "s", tag=name + "s", align_bytes=64)
            nc.vector.memset(planes[:].bitcast(I32), 0)
            runs = []
            for j, (g0, g1) in enumerate(head_runs):
                codes = keep.tile(
                    [P, g1 - g0, 1024], U8, name="%sc%d" % (name, j), tag="%sc%d" % (name, j), align_bytes=64
                )
                runs.append((g0, g1, codes, planes))
            first[name] = runs
        load_codes(first["x0"][0], x_src(0)[0])
        load_codes(first["w0"][0], w_src(0)[0])
        load_scales((0, PASSES, None, first["x0"][0][3]), x_src(0)[1])
        load_scales((0, PASSES, None, first["w0"][0][3]), w_src(0)[1])
        for j in (1, 2):
            load_codes(first["x0"][j], x_src(0)[0])
            load_codes(first["w0"][j], w_src(0)[0])
        xop[0] = [(codes, g - g0, planes, g) for g0, g1, codes, planes in first["x0"] for g in range(g0, g1)]
        wop[0] = [(codes, g - g0, planes, g) for g0, g1, codes, planes in first["w0"] for g in range(g0, g1)]

        eps = keep.tile([P, 1], F32, name="eps", tag="eps")
        nc.vector.memset(eps[:], EPS)
        warm = keep.tile([P, 1], F32, name="warm", tag="warm")
        nc.scalar.activation(out=warm[:], in_=eps[:], func=ACT.Abs_reciprocal_sqrt)
        ident = keep.tile([P, P], BF16, name="ident", tag="ident")
        make_identity(nc, ident[:])

        tab_sb = keep.tile([P, 1024], BF16, name="tab_sb", tag="tab_sb")
        b_sb = keep.tile([P, 2560], BF16, name="b_sb", tag="b_sb")

        w_runs = {}
        for n in range(1, BANKS):
            w_runs[n] = make_run("w%d" % n, 0, PASSES)
            wop[n] = by_pass([w_runs[n]])
        x_runs = {}
        for tb in range(1, BLOCKS):
            x_runs[tb] = make_run("x%d" % tb, 0, PASSES)
            xop[tb] = by_pass([x_runs[tb]])

        def load_w(n):
            load_scales(w_runs[n], w_src(n)[1])
            load_codes(w_runs[n], w_src(n)[0])

        def load_x(tb):
            load_scales(x_runs[tb], x_src(tb)[1])
            load_codes(x_runs[tb], x_src(tb)[0])

        load_w(1)
        nc.sync.dma_start(
            out=tab_sb[:, 0:256].rearrange("p (t j) -> p t j", t=4), in_=cos.rearrange("(t p) j -> p t j", p=P)
        )
        nc.sync.dma_start(
            out=tab_sb[:, 768:1024].rearrange("p (t j) -> p t j", t=4), in_=sin.rearrange("(t p) j -> p t j", p=P)
        )
        nc.sync.dma_start(out=tab_sb[:, 512:640], in_=qn_w.partition_broadcast(P))
        nc.sync.dma_start(out=tab_sb[:, 640:768], in_=kn_w.partition_broadcast(P))
        nc.sync.dma_start(out=b_sb[:, 0:2048], in_=bq.partition_broadcast(P))
        nc.sync.dma_start(out=b_sb[:, 2048:2560], in_=bk.partition_broadcast(P))
        for n in range(2, BANKS):
            load_w(n)
        load_x(1)

        nc.vector.tensor_scalar_mul(out=tab_sb[:, 256:512], in0=tab_sb[:, 768:1024], scalar1=-1.0)

        tabp = tab_pool.tile([P, 1024], BF16, name="tabp", tag="tabp")
        for w in range(WARM):
            nc.tensor.matmul(out=tabp[:, 0:512], lhsT=zeros[:, 0:128], rhs=zeros[:], start=True, stop=True)

        def mx_pass(acc, tb, i, n, g):
            xc, gx, xs, hx = xop[tb][g]
            wc, gw, ws, hw = wop[n][g]
            nc.tensor.matmul_mx(
                out=acc[:],
                lhsT=xc[:, gx, 256 * i : 256 * (i + 1)].bitcast(FP4X4),
                lhsT_scale=xs[:, hx, 128 * i : 128 * (i + 1)],
                rhs=wc[:, gw, :].bitcast(FP4X4),
                rhs_scale=ws[:, hw, :],
                start=(g == 0),
                stop=(g == PASSES - 1),
            )

        pairs = [(tb, n, q) for tb in range(BLOCKS) for n in range(BANKS) for q in range(2)]
        K = len(pairs)
        accs = {}
        v2s = {}
        abs_ = {}
        r2s = {}
        sss = {}
        rstds = {}
        y2s = {}

        def new_acc():
            acc = acc_pool.tile([P, 512], F32, name="acc", tag="acc")
            return acc

        def emit_mx(k):
            if k in accs:
                return
            tb, n, q = pairs[k]
            if k == 0:
                accs[0] = [new_acc(), new_acc()]
                accs[1] = [new_acc(), new_acc()]
                for g in range(PASSES):
                    for i in range(4):
                        mx_pass(accs[i // 2][i % 2], 0, i, 0, g)
                nc.tensor.matmul(out=tabp[:, 0:512], lhsT=ident[:], rhs=tab_sb[:, 0:512], start=True, stop=True)
                nc.tensor.matmul(out=tabp[:, 512:1024], lhsT=ident[:], rhs=tab_sb[:, 512:1024], start=True, stop=True)
                return
            accs[k] = [new_acc(), new_acc()]
            for u in range(2):
                for g in range(PASSES):
                    mx_pass(accs[k][u], tb, 2 * q + u, n, g)

        def alloc(k):
            v2s[k] = work.tile([P, 2, 512], F32, name="v2", tag="v2", bufs=3)
            abs_[k] = work.tile([P, 2, 2, 512], F32, name="ab", tag="ab", bufs=3)
            r2s[k] = work.tile([P, 2, 512], F32, name="r2", tag="r2", bufs=4)
            sss[k] = work.tile([P, 8], F32, name="ss", tag="ss", bufs=4)
            rstds[k] = work.tile([P, 8], F32, name="rstd", tag="rstd", bufs=4)
            y2s[k] = work.tile([P, 2, 512], F32, name="y2", tag="y2", bufs=3)

        def p1(k, u):
            tb, n, q = pairs[k]
            nc.vector.tensor_tensor(
                out=v2s[k][:, u, :].rearrange("p (h e j) -> p h e j", h=4, e=2),
                in0=accs[k][u][:].rearrange("p (h j e) -> p h e j", h=4, e=2),
                in1=b_sb[:, 512 * n : 512 * (n + 1)].rearrange("p (h j e) -> p h e j", h=4, e=2),
                op=ALU.add,
            )

        def halves(t3):
            return t3.rearrange("p u (h f j) -> p u h f j", h=4, f=2)

        def table(src, col, k, u0, nu, reps):
            q = pairs[k][2]
            t0 = 2 * q + u0
            return (
                src[:, col : col + 256]
                .rearrange("p (t j) -> p t j", t=4)[:, t0 : t0 + nu, :]
                .unsqueeze(2)
                .to_broadcast([P, nu, reps, 64])
            )

        def a(k, u0, nu):
            nc.vector.tensor_tensor(
                out=abs_[k][:, 0, u0 : u0 + nu, :].rearrange("p u (m j) -> p u m j", j=64),
                in0=v2s[k][:, u0 : u0 + nu, :].rearrange("p u (m j) -> p u m j", j=64),
                in1=table(tabp, 0, k, u0, nu, 8),
                op=ALU.mult,
            )

        def b0(k, u0, nu):
            nc.vector.tensor_tensor(
                out=halves(abs_[k][:, 1, u0 : u0 + nu, :])[:, :, :, 0, :],
                in0=halves(v2s[k][:, u0 : u0 + nu, :])[:, :, :, 1, :],
                in1=table(tabp, 256, k, u0, nu, 4),
                op=ALU.mult,
            )

        def b1(k, u0, nu, on_vector=False):
            eng = nc.vector if on_vector else nc.gpsimd
            eng.tensor_tensor(
                out=halves(abs_[k][:, 1, u0 : u0 + nu, :])[:, :, :, 1, :],
                in0=halves(v2s[k][:, u0 : u0 + nu, :])[:, :, :, 0, :],
                in1=table(tabp if on_vector else tab_sb, 768, k, u0, nu, 4),
                op=ALU.mult,
            )

        def plus(k, u0, nu, on_vector=False):
            eng = nc.vector if on_vector else nc.gpsimd
            eng.tensor_tensor(
                out=r2s[k][:, u0 : u0 + nu, :],
                in0=abs_[k][:, 0, u0 : u0 + nu, :],
                in1=abs_[k][:, 1, u0 : u0 + nu, :],
                op=ALU.add,
            )

        def squares(k, u0, nu):
            for u in range(u0, u0 + nu):
                for h in range(4):
                    junk = work.tile([P, 2, 128], BF16, name="junk", tag="junk", bufs=4)
                    nc.scalar.activation(
                        out=junk[:],
                        in_=abs_[k][:, :, u, 128 * h : 128 * (h + 1)],
                        func=ACT.Square,
                        accum_out=sss[k][:, 4 * u + h : 4 * u + h + 1],
                    )
            cols = slice(4 * u0, 4 * (u0 + nu))
            nc.scalar.activation(
                out=rstds[k][:, cols],
                in_=sss[k][:, cols],
                func=ACT.Abs_reciprocal_sqrt,
                scale=1.0 / 128.0,
                bias=eps[:, 0:1],
            )

        def final_head(k, m):
            wofs = 512 if pairs[k][1] < 4 else 640
            nc.vector.scalar_tensor_tensor(
                out=y2s[k][:, m // 4, 128 * (m % 4) : 128 * (m % 4 + 1)],
                in0=r2s[k][:, m // 4, 128 * (m % 4) : 128 * (m % 4 + 1)],
                scalar=rstds[k][:, m : m + 1],
                in1=tabp[:, wofs : wofs + 128],
                op0=ALU.mult,
                op1=ALU.mult,
            )

        def store(k, u0, nu):
            tb, n, q = pairs[k]
            r0 = 512 * tb + 256 * q + 128 * u0
            if n < 4:
                dst = q_rows[r0 : r0 + 128 * nu, 512 * n : 512 * (n + 1)]
            else:
                dst = k_rows[r0 : r0 + 128 * nu, :]
            nc.sync.dma_start(out=dst.rearrange("(u p) c -> p u c", p=P), in_=y2s[k][:, u0 : u0 + nu, :])

        UNITS = 2 * K
        FIRST_FINE = K - 3
        RAMP = UNITS - 8
        heads = [(k, m) for k in range(K) for m in range(8)]
        state = {"done": 0}

        def ready_slot(k, m):
            if k >= FIRST_FINE:
                return 2 * k + m // 4 + 3
            return 2 * k + 3

        def store_head(k, m):
            tb, n, q = pairs[k]
            r0 = 512 * tb + 256 * q + 128 * (m // 4)
            c0 = 128 * (m % 4)
            if n < 4:
                dst = q_rows[r0 : r0 + 128, 512 * n + c0 : 512 * n + c0 + 128]
            else:
                dst = k_rows[r0 : r0 + 128, c0 : c0 + 128]
            nc.sync.dma_start(out=dst, in_=y2s[k][:, m // 4, c0 : c0 + 128])

        def finals(slot, quota):
            for k, m in heads[state["done"] : state["done"] + quota]:
                assert ready_slot(k, m) <= slot
                final_head(k, m)
                if k == K - 1 and m >= 4:
                    store_head(k, m)
                elif k >= FIRST_FINE:
                    if m % 4 == 3:
                        store(k, m // 4, 1)
                elif m == 7:
                    store(k, 0, 2)
            state["done"] = state["done"] + quota

        for n in range(UNITS):
            c, u = divmod(n, 2)
            fine = c >= FIRST_FINE
            if u == 0:
                emit_mx(c)
                alloc(c)
            p1(c, u)
            if fine:
                if n < UNITS - 1:
                    b1(c, u, 1)
                if n > 2 * FIRST_FINE:
                    plus((n - 1) // 2, (n - 1) % 2, 1)
            elif u == 1:
                b1(c, 0, 2)
            if n >= 4:
                finals(n, 2)
            a(c, u, 1)
            b0(c, u, 1)
            if n == UNITS - 1:
                b1(c, u, 1, on_vector=True)
            if fine:
                squares(c, u, 1)
            elif u == 1:
                squares(c, 0, 2)
                plus(c, 0, 2)
            if n >= 4:
                finals(n, 3 if RAMP <= n < RAMP + 4 else 2)
            if u == 1 and c in (4, 8):
                load_x(c // 4 + 1)
        plus(K - 1, 1, 1)
        finals(UNITS + 2, len(heads) - state["done"])
